import numpy as np
import ml_dtypes


def mxq(x, axis, fmt="e4m3"):
    dtype, down = {"e4m3": (ml_dtypes.float8_e4m3fn, 7), "e5m2": (ml_dtypes.float8_e5m2, 14)}[fmt]
    v = np.moveaxis(np.asarray(x, np.float32).astype(ml_dtypes.bfloat16).astype(np.float64), axis, -1)
    blocks = v.reshape(v.shape[:-1] + (-1, 32))
    amax = np.abs(blocks).max(-1, keepdims=True)
    byte = np.maximum(np.where(amax > 0, np.frexp(amax)[1] - 1 + 127, 0) - down, 1)
    scale = np.exp2(byte - 127.0)
    codes = (blocks / scale).astype(np.float32).astype(dtype).astype(np.float64)
    return np.moveaxis((codes * scale).reshape(v.shape), -1, axis)


WIDE = False


def mx_kscale(k):
    if not WIDE:
        return np.ones(k)
    levels = np.array([10, -10, 5, -5, 0])
    if k % 512:
        return np.exp2(np.random.permutation(np.resize(levels, k // 32))).repeat(32)
    a = np.empty((k // 512, 16))
    for p in range(k // 512):
        a[p, :8] = np.random.permutation(np.resize(levels, 8))
        for g in range(8):
            far = levels[np.abs(levels - a[p, g]) >= 10]
            a[p, g + 8] = far[np.random.randint(len(far))]
    return np.exp2(a.ravel()).repeat(32)


BF16 = ml_dtypes.bfloat16


def bf(x):
    return np.asarray(x, np.float32).astype(BF16)


def f64(x):
    return np.asarray(x).astype(np.float64)


NA, NB, H = 1024, 1024, 512


def sigmoid(v):
    return 1.0 / (1.0 + np.exp(-v))


def setup_inputs():
    s, t = mx_kscale(H), mx_kscale(H)
    return {"y_a": bf(np.random.standard_normal((NA, H)) * 0.25 / t),
            "y_b": bf(np.random.standard_normal((NB, H)) * s),
            "W": bf(np.random.standard_normal((H, H)) * 6.0 / H * t[:, None] / s[None, :]),
            "b": bf(np.random.standard_normal(H) * 5.0 / np.sqrt(H) * t)}


def reference(y_a, y_b, W, b):
    proj = (mxq(f64(y_b), 1, "e4m3") @ mxq(f64(W), 1, "e4m3").T) + f64(b)
    scores = mxq(f64(y_a), 1, "e4m3") @ mxq(proj, 1, "e4m3").T
    s = np.sum(sigmoid(scores), axis=1) / y_a.shape[1]
    return np.broadcast_to(s[:, None], y_a.shape).copy()

@@ -1,0 +1,254 @@
+from contextlib import ExitStack
+
+import concourse.mybir as mybir
+from concourse.masks import make_identity
+
+F32 = mybir.dt.float32
+BF16 = mybir.dt.bfloat16
+U32 = mybir.dt.uint32
+U8 = mybir.dt.uint8
+FP8X4 = mybir.dt.float8_e4m3fn_x4
+ACT = mybir.ActivationFunctionType
+ALU = mybir.AluOpType
+
+P = 128
+NA, NB, H = 1024, 1024, 512
+FLOPS = 2 * NB * H * H + 2 * NA * NB * H
+WIDTHS = [512, 512]
+NCH = 2
+
+
+def tile_miscore_kernel(tc, y_a, y_b, W, b, out):
+    nc = tc.nc
+    with ExitStack() as ctx:
+        keep = ctx.enter_context(tc.tile_pool(name="keep", bufs=1))
+        outp = ctx.enter_context(tc.tile_pool(name="outp", bufs=4))
+        psum = ctx.enter_context(tc.psum_pool(name="psum", bufs=1))
+        ctx.enter_context(tc.manual_schedule())
+
+        ya_v = y_a.rearrange("(p r) o -> p r o", r=8)
+        out_v = out.rearrange("(p r) k -> p r k", r=8)
+        W_v = W.rearrange("(p t) i -> p t i", t=4)
+        w0 = keep.tile([P, 1024], BF16, name="w0")
+        nc.sync.dma_start(out=w0[:, :].rearrange("p (t i) -> p t i", t=2), in_=W_v[:, 0 : 2, :])
+        w1 = keep.tile([P, 1024], BF16, name="w1")
+        nc.sync.dma_start(out=w1[:, :].rearrange("p (t i) -> p t i", t=2), in_=W_v[:, 2 : 4, :])
+        yb0 = keep.tile([P, 1024], BF16, name="yb0")
+        nc.sync.dma_start(out=yb0[:, :], in_=y_b[0 : 256, :].rearrange("(p r) i -> p (r i)", r=2))
+        yb1 = keep.tile([P, 1024], BF16, name="yb1")
+        nc.sync.dma_start(out=yb1[:, :], in_=y_b[256 : 512, :].rearrange("(p r) i -> p (r i)", r=2))
+        ya0 = keep.tile([P, 2048], BF16, name="ya0")
+        nc.sync.dma_start(out=ya0[:, :].rearrange("p (r o) -> p r o", r=4), in_=ya_v[:, 0 : 4, :])
+        yb2 = keep.tile([P, 2048], BF16, name="yb2")
+        nc.sync.dma_start(out=yb2[:, :], in_=y_b[512 : 1024, :].rearrange("(p r) i -> p (r i)", r=4))
+        ya1 = keep.tile([P, 2048], BF16, name="ya1")
+        nc.sync.dma_start(out=ya1[:, :].rearrange("p (r o) -> p r o", r=4), in_=ya_v[:, 4 : 8, :])
+        srcs = {"w0": (w0, 0), "w1": (w1, 0), "b0": (yb0, 0), "b1": (yb1, 0), "a0": (ya0, 0), "a1": (ya0, 1), "b2": (yb2, 0), "b3": (yb2, 1), "a2": (ya1, 0), "a3": (ya1, 1)}
+        b_bf = keep.tile([P, 4], BF16, name="b_bf")
+        nc.scalar.dma_start(out=b_bf[:, :], in_=b.rearrange("(p t) -> p t", t=4))
+
+        zb = keep.tile([P, 512], BF16, name="zb")
+        nc.vector.memset(zb[:, :], 0.0)
+        warm = keep.tile([P, 1], F32, name="warm")
+        warm2 = keep.tile([P, 1], F32, name="warm2")
+        nc.vector.memset(warm[:, :], 0.0)
+        nc.scalar.activation(out=warm2[:, :], in_=warm[:, :], func=ACT.Sigmoid)
+        ident = keep.tile([P, P], F32, name="ident")
+        make_identity(nc, ident[:, :])
+        cdiv = keep.tile([P, H], F32, name="cdiv")
+        nc.vector.memset(cdiv[:, :], 1.0 / H)
+        bias = keep.tile([P, 4], F32, name="bias")
+        bias_b = bias[:, :].unsqueeze(1).to_broadcast([P, P, 4])
+        g2 = [keep.tile([P, 4 * WIDTHS[c]], BF16, name="g2c%d" % c, align_bytes=64) for c in range(NCH)]
+        acc = keep.tile([P, 8 * NCH], F32, name="acc")
+        acc0 = keep.tile([P, 8], F32, name="acc0")
+        junk = keep.tile([P, 512], BF16, name="junk")
+        tp, gr, qz, pj, pq, sc = {}, {}, {}, {}, {}, {}
+        dmy = psum.tile([P, 512], F32, name="dmy", tag="bank7")
+
+        def dummy(bank):
+            nc.tensor.matmul(out=bank[:, :], lhsT=zb[:, 0:128], rhs=zb[:, :], start=True, stop=True)
+
+        def bank_tile(n, name):
+            return psum.tile([P, 512], F32, name=name, tag="bank%d" % n)
+
+        def transposes(x, k, n):
+            src, pair = srcs["%s%d" % (x, k)]
+            bank = bank_tile(n, "t%s%d" % (x, k))
+            s32 = src[:, :].bitcast(F32)
+            for q in range(4):
+                c0 = 512 * pair + 256 * (q // 2) + q % 2
+                nc.tensor.transpose(bank[:, 128 * q : 128 * (q + 1)], s32[:, c0 : c0 + 255 : 2], ident[:, :])
+            return bank
+
+        def copy_out(eng, bank, name):
+            g = keep.tile([P, 1024], BF16, name=name, align_bytes=64)
+            dst = g[:, :].bitcast(F32).rearrange("p (r c u) -> p r c u", r=2, u=2)
+            src = bank[:, :].rearrange("p (r u c) -> p r c u", r=2, u=2)
+            if eng == "v":
+                nc.vector.tensor_copy(out=dst, in_=src)
+            else:
+                nc.scalar.copy(out=dst, in_=src)
+            return g
+
+        def quantise(g, width, name):
+            codes = keep.tile([P, width // 4], U32, name=name + "c", align_bytes=64)
+            scales = keep.tile([P, width // 4], U8, name=name + "s", align_bytes=64)
+            nc.vector.quantize_mx(out=codes[:, :].bitcast(FP8X4), scales=scales[:, :], in_=g[:, :])
+            return codes, scales
+
+        def cols(op, k):
+            codes, scales = op
+            return codes[:, 128 * k : 128 * (k + 1)].bitcast(FP8X4), scales[:, 128 * k : 128 * (k + 1)]
+
+        def proj_mm(jc, n):
+            bank = bank_tile(n, "pj%d" % jc)
+            rhs, rhs_s = cols(qz["b%d" % (jc // 2)], jc % 2)
+            for t in range(4):
+                lhsT, lhsT_s = cols(qz["w%d" % (t // 2)], t % 2)
+                nc.tensor.matmul_mx(
+                    out=bank[:, 128 * t : 128 * (t + 1)],
+                    lhsT=lhsT, lhsT_scale=lhsT_s, rhs=rhs, rhs_scale=rhs_s,
+                    start=True, stop=True,
+                )
+            return bank
+
+        def proj_add(bank, c, k):
+            nc.vector.tensor_tensor(
+                out=g2[c][:, 512 * k : 512 * (k + 1)].rearrange("p (j t) -> p j t", t=4),
+                in0=bank[:, :].rearrange("p (t j) -> p j t", t=4),
+                in1=bias_b,
+                op=ALU.add,
+            )
+
+        def score_mm(c, r, n):
+            bank = bank_tile(n, "sc%d_%d" % (c, r))
+            lhsT, lhsT_s = cols(qz["a%d" % (r // 2)], r % 2)
+            nc.tensor.matmul_mx(
+                out=bank[:, 0 : WIDTHS[c]], lhsT=lhsT, lhsT_scale=lhsT_s,
+                rhs=pq[c][0][:, :].bitcast(FP8X4), rhs_scale=pq[c][1][:, :],
+                start=True, stop=True,
+            )
+            return bank
+
+        def score_sig(c, r):
+            nc.scalar.activation(
+                out=junk[:, 0 : WIDTHS[c]], in_=sc[(c, r)][:, 0 : WIDTHS[c]], func=ACT.Sigmoid,
+                accum_out=acc[:, 8 * c + r : 8 * c + r + 1],
+            )
+
+        def early_sums():
+            if NCH == 2:
+                nc.vector.tensor_scalar(out=acc0[:, :], in0=acc[:, 0:8], scalar1=1.0 / H, scalar2=None, op0=ALU.mult)
+            else:
+                nc.vector.tensor_tensor(out=acc0[:, :], in0=acc[:, 0:8], in1=acc[:, 8:16], op=ALU.add)
+                nc.vector.tensor_scalar(out=acc0[:, :], in0=acc0[:, :], scalar1=1.0 / H, scalar2=None, op0=ALU.mult)
+
+        def finish(r):
+            o_sb = outp.tile([P, H], F32, name="o_sb")
+            c = 8 * (NCH - 1) + r
+            nc.vector.tensor_scalar(
+                out=o_sb[:, :], in0=cdiv[:, :],
+                scalar1=acc[:, c : c + 1], scalar2=acc0[:, r : r + 1],
+                op0=ALU.mult, op1=ALU.add,
+            )
+            nc.sync.dma_start(out=out_v[:, r, :], in_=o_sb[:, :])
+
+        dummy(dmy)
+        dummy(dmy)
+        dummy(dmy)
+        dummy(dmy)
+        dummy(dmy)
+        dummy(dmy)
+        tp["w0"] = transposes("w", 0, 0)
+        tp["w1"] = transposes("w", 1, 1)
+        dummy(dmy)
+        gr["w0"] = copy_out("s", tp["w0"], "gw0")
+        tp["b0"] = transposes("b", 0, 2)
+        gr["w1"] = copy_out("v", tp["w1"], "gw1")
+        tp["b1"] = transposes("b", 1, 3)
+        dummy(dmy)
+        qz["w0"] = quantise(gr["w0"], 1024, "qw0")
+        gr["b0"] = copy_out("s", tp["b0"], "gb0")
+        qz["w1"] = quantise(gr["w1"], 1024, "qw1")
+        gr["b1"] = copy_out("s", tp["b1"], "gb1")
+        qz["b0"] = quantise(gr["b0"], 1024, "qb0")
+        tp["a0"] = transposes("a", 0, 4)
+        qz["b1"] = quantise(gr["b1"], 1024, "qb1")
+        pj[0] = proj_mm(0, 5)
+        gr["a0"] = copy_out("s", tp["a0"], "ga0")
+        pj[1] = proj_mm(1, 6)
+        nc.vector.tensor_copy(out=bias[:, :], in_=b_bf[:, :])
+        proj_add(pj[0], 0, 0)
+        pj[2] = proj_mm(2, 7)
+        proj_add(pj[1], 0, 1)
+        tp["b2"] = transposes("b", 2, 0)
+        qz["a0"] = quantise(gr["a0"], 1024, "qa0")
+        proj_add(pj[2], 0, 2)
+        tp["b3"] = transposes("b", 3, 1)
+        gr["b2"] = copy_out("s", tp["b2"], "gb2")
+        pj[3] = proj_mm(3, 2)
+        gr["b3"] = copy_out("s", tp["b3"], "gb3")
+        qz["b2"] = quantise(gr["b2"], 1024, "qb2")
+        tp["a1"] = transposes("a", 1, 3)
+        proj_add(pj[3], 0, 3)
+        tp["a2"] = transposes("a", 2, 4)
+        gr["a1"] = copy_out("s", tp["a1"], "ga1")
+        tp["a3"] = transposes("a", 3, 5)
+        pq[0] = quantise(g2[0], 2048, "pq0")
+        pj[4] = proj_mm(4, 6)
+        gr["a2"] = copy_out("s", tp["a2"], "ga2")
+        pj[5] = proj_mm(5, 7)
+        qz["b3"] = quantise(gr["b3"], 1024, "qb3")
+        qz["a1"] = quantise(gr["a1"], 1024, "qa1")
+        sc[(0, 0)] = score_mm(0, 0, 0)
+        gr["a3"] = copy_out("s", tp["a3"], "ga3")
+        proj_add(pj[4], 1, 0)
+        sc[(0, 1)] = score_mm(0, 1, 1)
+        sc[(0, 2)] = score_mm(0, 2, 2)
+        score_sig(0, 0)
+        qz["a2"] = quantise(gr["a2"], 1024, "qa2")
+        sc[(0, 3)] = score_mm(0, 3, 3)
+        proj_add(pj[5], 1, 1)
+        pj[6] = proj_mm(6, 4)
+        score_sig(0, 1)
+        pj[7] = proj_mm(7, 5)
+        qz["a3"] = quantise(gr["a3"], 1024, "qa3")
+        sc[(0, 4)] = score_mm(0, 4, 6)
+        score_sig(0, 2)
+        proj_add(pj[6], 1, 2)
+        sc[(0, 5)] = score_mm(0, 5, 7)
+        score_sig(0, 3)
+        sc[(0, 6)] = score_mm(0, 6, 0)
+        proj_add(pj[7], 1, 3)
+        sc[(0, 7)] = score_mm(0, 7, 1)
+        score_sig(0, 4)
+        pq[1] = quantise(g2[1], 2048, "pq1")
+        score_sig(0, 5)
+        score_sig(0, 6)
+        sc[(1, 0)] = score_mm(1, 0, 2)
+        sc[(1, 1)] = score_mm(1, 1, 3)
+        sc[(1, 2)] = score_mm(1, 2, 4)
+        score_sig(0, 7)
+        sc[(1, 3)] = score_mm(1, 3, 5)
+        sc[(1, 4)] = score_mm(1, 4, 6)
+        score_sig(1, 0)
+        early_sums()
+        sc[(1, 5)] = score_mm(1, 5, 7)
+        sc[(1, 6)] = score_mm(1, 6, 0)
+        score_sig(1, 1)
+        finish(0)
+        sc[(1, 7)] = score_mm(1, 7, 1)
+        score_sig(1, 2)
+        finish(1)
+        score_sig(1, 3)
+        finish(2)
+        score_sig(1, 4)
+        finish(3)
+        score_sig(1, 5)
+        finish(4)
+        score_sig(1, 6)
+        finish(5)
+        score_sig(1, 7)
+        finish(6)
+        finish(7)

@@ -22,7 +22,7 @@ def tile_miscore_kernel(tc, y_a, y_b, W, b, out):
     nc = tc.nc
     with ExitStack() as ctx:
         keep = ctx.enter_context(tc.tile_pool(name="keep", bufs=1))
-        outp = ctx.enter_context(tc.tile_pool(name="outp", bufs=4))
+        outp = ctx.enter_context(tc.tile_pool(name="outp", bufs=8))
         psum = ctx.enter_context(tc.psum_pool(name="psum", bufs=1))
         ctx.enter_context(tc.manual_schedule())
 

@@ -14,8 +14,6 @@ ALU = mybir.AluOpType
 P = 128
 NA, NB, H = 1024, 1024, 512
 FLOPS = 2 * NB * H * H + 2 * NA * NB * H
-WIDTHS = [512, 512]
-NCH = 2
 
 
 def tile_miscore_kernel(tc, y_a, y_b, W, b, out):
@@ -29,23 +27,21 @@ def tile_miscore_kernel(tc, y_a, y_b, W, b, out):
         ya_v = y_a.rearrange("(p r) o -> p r o", r=8)
         out_v = out.rearrange("(p r) k -> p r k", r=8)
         W_v = W.rearrange("(p t) i -> p t i", t=4)
-        w0 = keep.tile([P, 1024], BF16, name="w0")
-        nc.sync.dma_start(out=w0[:, :].rearrange("p (t i) -> p t i", t=2), in_=W_v[:, 0 : 2, :])
-        w1 = keep.tile([P, 1024], BF16, name="w1")
-        nc.sync.dma_start(out=w1[:, :].rearrange("p (t i) -> p t i", t=2), in_=W_v[:, 2 : 4, :])
-        yb0 = keep.tile([P, 1024], BF16, name="yb0")
-        nc.sync.dma_start(out=yb0[:, :], in_=y_b[0 : 256, :].rearrange("(p r) i -> p (r i)", r=2))
-        yb1 = keep.tile([P, 1024], BF16, name="yb1")
-        nc.sync.dma_start(out=yb1[:, :], in_=y_b[256 : 512, :].rearrange("(p r) i -> p (r i)", r=2))
-        ya0 = keep.tile([P, 2048], BF16, name="ya0")
-        nc.sync.dma_start(out=ya0[:, :].rearrange("p (r o) -> p r o", r=4), in_=ya_v[:, 0 : 4, :])
-        yb2 = keep.tile([P, 2048], BF16, name="yb2")
-        nc.sync.dma_start(out=yb2[:, :], in_=y_b[512 : 1024, :].rearrange("(p r) i -> p (r i)", r=4))
-        ya1 = keep.tile([P, 2048], BF16, name="ya1")
-        nc.sync.dma_start(out=ya1[:, :].rearrange("p (r o) -> p r o", r=4), in_=ya_v[:, 4 : 8, :])
-        srcs = {"w0": (w0, 0), "w1": (w1, 0), "b0": (yb0, 0), "b1": (yb1, 0), "a0": (ya0, 0), "a1": (ya0, 1), "b2": (yb2, 0), "b3": (yb2, 1), "a2": (ya1, 0), "a3": (ya1, 1)}
+
+        def load(name, rows, source):
+            x = keep.tile([P, 512 * rows], BF16, name=name)
+            nc.sync.dma_start(out=x[:, :].rearrange("p (r k) -> p r k", r=rows), in_=source)
+            return x
+
         b_bf = keep.tile([P, 4], BF16, name="b_bf")
         nc.scalar.dma_start(out=b_bf[:, :], in_=b.rearrange("(p t) -> p t", t=4))
+        yb_v = [y_b[256 * c : 256 * (c + 1), :].rearrange("(p r) i -> p r i", r=2) for c in range(4)]
+        srcs = {}
+        for x, source in (
+            ("w0", W_v[:, 0:2, :]), ("w1", W_v[:, 2:4, :]), ("b0", yb_v[0]), ("a0", ya_v[:, 0:2, :]), ("b1", yb_v[1]),
+            ("a1", ya_v[:, 2:4, :]), ("b2", yb_v[2]), ("a2", ya_v[:, 4:6, :]), ("b3", yb_v[3]), ("a3", ya_v[:, 6:8, :]),
+        ):
+            srcs[x] = load(x, 2, source)
 
         zb = keep.tile([P, 512], BF16, name="zb")
         nc.vector.memset(zb[:, :], 0.0)
@@ -59,49 +55,58 @@ def tile_miscore_kernel(tc, y_a, y_b, W, b, out):
         nc.vector.memset(cdiv[:, :], 1.0 / H)
         bias = keep.tile([P, 4], F32, name="bias")
         bias_b = bias[:, :].unsqueeze(1).to_broadcast([P, P, 4])
-        g2 = [keep.tile([P, 4 * WIDTHS[c]], BF16, name="g2c%d" % c, align_bytes=64) for c in range(NCH)]
-        acc = keep.tile([P, 8 * NCH], F32, name="acc")
+        acc = keep.tile([P, 20], F32, name="acc")
         acc0 = keep.tile([P, 8], F32, name="acc0")
         junk = keep.tile([P, 512], BF16, name="junk")
-        tp, gr, qz, pj, pq, sc = {}, {}, {}, {}, {}, {}
-        dmy = psum.tile([P, 512], F32, name="dmy", tag="bank7")
-
-        def dummy(bank):
-            nc.tensor.matmul(out=bank[:, :], lhsT=zb[:, 0:128], rhs=zb[:, :], start=True, stop=True)
+        pc = keep.tile([P, NB], U32, name="pc", align_bytes=64)
+        ps = keep.tile([P, NB], U8, name="ps", align_bytes=64)
+        tp, gr, qz, pj, sc = {}, {}, {}, {}, {}
+        g2 = {}
 
         def bank_tile(n, name):
             return psum.tile([P, 512], F32, name=name, tag="bank%d" % n)
 
-        def transposes(x, k, n):
-            src, pair = srcs["%s%d" % (x, k)]
-            bank = bank_tile(n, "t%s%d" % (x, k))
-            s32 = src[:, :].bitcast(F32)
+        dmy = bank_tile(7, "dmy")
+
+        def dummy():
+            nc.tensor.matmul(out=dmy[:, :], lhsT=zb[:, 0:128], rhs=zb[:, :], start=True, stop=True)
+
+        def T(x, n):
+            bank = bank_tile(n, "t" + x)
+            s32 = srcs[x][:, :].bitcast(F32)
             for q in range(4):
-                c0 = 512 * pair + 256 * (q // 2) + q % 2
+                c0 = 256 * (q // 2) + q % 2
                 nc.tensor.transpose(bank[:, 128 * q : 128 * (q + 1)], s32[:, c0 : c0 + 255 : 2], ident[:, :])
-            return bank
+            tp[x] = bank
 
-        def copy_out(eng, bank, name):
-            g = keep.tile([P, 1024], BF16, name=name, align_bytes=64)
-            dst = g[:, :].bitcast(F32).rearrange("p (r c u) -> p r c u", r=2, u=2)
-            src = bank[:, :].rearrange("p (r u c) -> p r c u", r=2, u=2)
-            if eng == "v":
-                nc.vector.tensor_copy(out=dst, in_=src)
-            else:
-                nc.scalar.copy(out=dst, in_=src)
-            return g
+        def C(x, eng, *halves):
+            if x not in gr:
+                gr[x] = keep.tile([P, 1024], BF16, name="g" + x, align_bytes=64)
+            for r0, r1 in [(h, h + 1) for h in halves] or [(0, 2)]:
+                dst = gr[x][:, 512 * r0 : 512 * r1].bitcast(F32).rearrange("p (r c u) -> p r c u", c=128, u=2)
+                src = tp[x][:, 256 * r0 : 256 * r1].rearrange("p (r u c) -> p r c u", u=2, c=128)
+                if eng == "v":
+                    nc.vector.tensor_copy(out=dst, in_=src)
+                else:
+                    nc.scalar.copy(out=dst, in_=src)
 
-        def quantise(g, width, name):
-            codes = keep.tile([P, width // 4], U32, name=name + "c", align_bytes=64)
-            scales = keep.tile([P, width // 4], U8, name=name + "s", align_bytes=64)
-            nc.vector.quantize_mx(out=codes[:, :].bitcast(FP8X4), scales=scales[:, :], in_=g[:, :])
-            return codes, scales
+        def Q(x, *halves):
+            if x not in qz:
+                codes = keep.tile([P, 256], U32, name="c" + x, align_bytes=64)
+                scales = keep.tile([P, 256], U8, name="s" + x, align_bytes=64)
+                qz[x] = (codes, scales)
+            codes, scales = qz[x]
+            for r0, r1 in [(h, h + 1) for h in halves] or [(0, 2)]:
+                cs = slice(128 * r0, 128 * r1)
+                nc.vector.quantize_mx(
+                    out=codes[:, cs].bitcast(FP8X4), scales=scales[:, cs], in_=gr[x][:, 512 * r0 : 512 * r1]
+                )
 
         def cols(op, k):
             codes, scales = op
             return codes[:, 128 * k : 128 * (k + 1)].bitcast(FP8X4), scales[:, 128 * k : 128 * (k + 1)]
 
-        def proj_mm(jc, n):
+        def PJ(jc, n):
             bank = bank_tile(n, "pj%d" % jc)
             rhs, rhs_s = cols(qz["b%d" % (jc // 2)], jc % 2)
             for t in range(4):
@@ -111,144 +116,144 @@ def tile_miscore_kernel(tc, y_a, y_b, W, b, out):
                     lhsT=lhsT, lhsT_scale=lhsT_s, rhs=rhs, rhs_scale=rhs_s,
                     start=True, stop=True,
                 )
-            return bank
+            pj[jc] = bank
 
-        def proj_add(bank, c, k):
+        def ADD(jc):
+            c, k = jc // 2, jc % 2
+            if k == 0:
+                g2[c] = keep.tile([P, 1024], BF16, name="g2c%d" % c, align_bytes=64)
             nc.vector.tensor_tensor(
                 out=g2[c][:, 512 * k : 512 * (k + 1)].rearrange("p (j t) -> p j t", t=4),
-                in0=bank[:, :].rearrange("p (t j) -> p j t", t=4),
+                in0=pj[jc][:, :].rearrange("p (t j) -> p j t", t=4),
                 in1=bias_b,
                 op=ALU.add,
             )
 
-        def score_mm(c, r, n):
-            bank = bank_tile(n, "sc%d_%d" % (c, r))
+        def PQ(c):
+            nc.vector.quantize_mx(
+                out=pc[:, 256 * c : 256 * (c + 1)].bitcast(FP8X4),
+                scales=ps[:, 256 * c : 256 * (c + 1)],
+                in_=g2[c][:, :],
+            )
+
+        def S(r, c, w, n):
+            bank = bank_tile(n, "sc%d_%d" % (r, c))
             lhsT, lhsT_s = cols(qz["a%d" % (r // 2)], r % 2)
             nc.tensor.matmul_mx(
-                out=bank[:, 0 : WIDTHS[c]], lhsT=lhsT, lhsT_scale=lhsT_s,
-                rhs=pq[c][0][:, :].bitcast(FP8X4), rhs_scale=pq[c][1][:, :],
+                out=bank[:, 0 : 256 * w], lhsT=lhsT, lhsT_scale=lhsT_s,
+                rhs=pc[:, 256 * c : 256 * (c + w)].bitcast(FP8X4), rhs_scale=ps[:, 256 * c : 256 * (c + w)],
                 start=True, stop=True,
             )
-            return bank
+            sc[(r, c)] = (bank, w)
 
-        def score_sig(c, r):
+        def SIG(r, c, col):
+            bank, w = sc[(r, c)]
             nc.scalar.activation(
-                out=junk[:, 0 : WIDTHS[c]], in_=sc[(c, r)][:, 0 : WIDTHS[c]], func=ACT.Sigmoid,
-                accum_out=acc[:, 8 * c + r : 8 * c + r + 1],
+                out=junk[:, 0 : 256 * w], in_=bank[:, 0 : 256 * w], func=ACT.Sigmoid,
+                accum_out=acc[:, col : col + 1],
             )
-
-        def early_sums():
-            if NCH == 2:
-                nc.vector.tensor_scalar(out=acc0[:, :], in0=acc[:, 0:8], scalar1=1.0 / H, scalar2=None, op0=ALU.mult)
-            else:
-                nc.vector.tensor_tensor(out=acc0[:, :], in0=acc[:, 0:8], in1=acc[:, 8:16], op=ALU.add)
-                nc.vector.tensor_scalar(out=acc0[:, :], in0=acc0[:, :], scalar1=1.0 / H, scalar2=None, op0=ALU.mult)
 
         def finish(r):
             o_sb = outp.tile([P, H], F32, name="o_sb")
-            c = 8 * (NCH - 1) + r
             nc.vector.tensor_scalar(
                 out=o_sb[:, :], in0=cdiv[:, :],
-                scalar1=acc[:, c : c + 1], scalar2=acc0[:, r : r + 1],
+                scalar1=acc[:, r : r + 1], scalar2=acc0[:, r : r + 1],
                 op0=ALU.mult, op1=ALU.add,
             )
             nc.sync.dma_start(out=out_v[:, r, :], in_=o_sb[:, :])
 
-        dummy(dmy)
-        dummy(dmy)
-        dummy(dmy)
-        dummy(dmy)
-        dummy(dmy)
-        dummy(dmy)
-        tp["w0"] = transposes("w", 0, 0)
-        tp["w1"] = transposes("w", 1, 1)
-        dummy(dmy)
-        gr["w0"] = copy_out("s", tp["w0"], "gw0")
-        tp["b0"] = transposes("b", 0, 2)
-        gr["w1"] = copy_out("v", tp["w1"], "gw1")
-        tp["b1"] = transposes("b", 1, 3)
-        dummy(dmy)
-        qz["w0"] = quantise(gr["w0"], 1024, "qw0")
-        gr["b0"] = copy_out("s", tp["b0"], "gb0")
-        qz["w1"] = quantise(gr["w1"], 1024, "qw1")
-        gr["b1"] = copy_out("s", tp["b1"], "gb1")
-        qz["b0"] = quantise(gr["b0"], 1024, "qb0")
-        tp["a0"] = transposes("a", 0, 4)
-        qz["b1"] = quantise(gr["b1"], 1024, "qb1")
-        pj[0] = proj_mm(0, 5)
-        gr["a0"] = copy_out("s", tp["a0"], "ga0")
-        pj[1] = proj_mm(1, 6)
         nc.vector.tensor_copy(out=bias[:, :], in_=b_bf[:, :])
-        proj_add(pj[0], 0, 0)
-        pj[2] = proj_mm(2, 7)
-        proj_add(pj[1], 0, 1)
-        tp["b2"] = transposes("b", 2, 0)
-        qz["a0"] = quantise(gr["a0"], 1024, "qa0")
-        proj_add(pj[2], 0, 2)
-        tp["b3"] = transposes("b", 3, 1)
-        gr["b2"] = copy_out("s", tp["b2"], "gb2")
-        pj[3] = proj_mm(3, 2)
-        gr["b3"] = copy_out("s", tp["b3"], "gb3")
-        qz["b2"] = quantise(gr["b2"], 1024, "qb2")
-        tp["a1"] = transposes("a", 1, 3)
-        proj_add(pj[3], 0, 3)
-        tp["a2"] = transposes("a", 2, 4)
-        gr["a1"] = copy_out("s", tp["a1"], "ga1")
-        tp["a3"] = transposes("a", 3, 5)
-        pq[0] = quantise(g2[0], 2048, "pq0")
-        pj[4] = proj_mm(4, 6)
-        gr["a2"] = copy_out("s", tp["a2"], "ga2")
-        pj[5] = proj_mm(5, 7)
-        qz["b3"] = quantise(gr["b3"], 1024, "qb3")
-        qz["a1"] = quantise(gr["a1"], 1024, "qa1")
-        sc[(0, 0)] = score_mm(0, 0, 0)
-        gr["a3"] = copy_out("s", tp["a3"], "ga3")
-        proj_add(pj[4], 1, 0)
-        sc[(0, 1)] = score_mm(0, 1, 1)
-        sc[(0, 2)] = score_mm(0, 2, 2)
-        score_sig(0, 0)
-        qz["a2"] = quantise(gr["a2"], 1024, "qa2")
-        sc[(0, 3)] = score_mm(0, 3, 3)
-        proj_add(pj[5], 1, 1)
-        pj[6] = proj_mm(6, 4)
-        score_sig(0, 1)
-        pj[7] = proj_mm(7, 5)
-        qz["a3"] = quantise(gr["a3"], 1024, "qa3")
-        sc[(0, 4)] = score_mm(0, 4, 6)
-        score_sig(0, 2)
-        proj_add(pj[6], 1, 2)
-        sc[(0, 5)] = score_mm(0, 5, 7)
-        score_sig(0, 3)
-        sc[(0, 6)] = score_mm(0, 6, 0)
-        proj_add(pj[7], 1, 3)
-        sc[(0, 7)] = score_mm(0, 7, 1)
-        score_sig(0, 4)
-        pq[1] = quantise(g2[1], 2048, "pq1")
-        score_sig(0, 5)
-        score_sig(0, 6)
-        sc[(1, 0)] = score_mm(1, 0, 2)
-        sc[(1, 1)] = score_mm(1, 1, 3)
-        sc[(1, 2)] = score_mm(1, 2, 4)
-        score_sig(0, 7)
-        sc[(1, 3)] = score_mm(1, 3, 5)
-        sc[(1, 4)] = score_mm(1, 4, 6)
-        score_sig(1, 0)
-        early_sums()
-        sc[(1, 5)] = score_mm(1, 5, 7)
-        sc[(1, 6)] = score_mm(1, 6, 0)
-        score_sig(1, 1)
-        finish(0)
-        sc[(1, 7)] = score_mm(1, 7, 1)
-        score_sig(1, 2)
-        finish(1)
-        score_sig(1, 3)
-        finish(2)
-        score_sig(1, 4)
-        finish(3)
-        score_sig(1, 5)
-        finish(4)
-        score_sig(1, 6)
-        finish(5)
-        score_sig(1, 7)
-        finish(6)
-        finish(7)
+        for i in range(4):
+            dummy()
+        T("w0", 0)
+        C("w0", "s", 0)
+        C("w0", "s", 1)
+        T("w1", 1)
+        C("w1", "v", 0)
+        C("w1", "v", 1)
+        dummy()
+        T("b0", 2)
+        C("b0", "s", 0)
+        Q("w0")
+        C("b0", "s", 1)
+        Q("w1")
+        T("a0", 3)
+        C("a0", "s")
+        Q("b0", 0)
+        Q("b0", 1)
+        dummy()
+        T("b1", 6)
+        PJ(0, 4)
+        PJ(1, 5)
+        C("b1", "s")
+        ADD(0)
+        T("a1", 7)
+        C("a1", "s")
+        T("b2", 0)
+        C("b2", "s")
+        Q("b1")
+        ADD(1)
+        PJ(2, 1)
+        PJ(3, 2)
+        Q("a0")
+        PQ(0)
+        S(0, 0, 1, 3)
+        S(1, 0, 1, 4)
+        T("a2", 6)
+        SIG(0, 0, 8)
+        SIG(1, 0, 9)
+        C("a2", "s")
+        Q("a1")
+        ADD(2)
+        S(2, 0, 1, 5)
+        S(3, 0, 1, 7)
+        SIG(2, 0, 10)
+        SIG(3, 0, 11)
+        Q("b2")
+        ADD(3)
+        T("b3", 0)
+        C("b3", "s")
+        PJ(4, 1)
+        PJ(5, 2)
+        T("a3", 6)
+        Q("a2")
+        PQ(1)
+        ADD(4)
+        S(0, 1, 1, 3)
+        S(1, 1, 1, 4)
+        S(2, 1, 1, 5)
+        S(3, 1, 1, 7)
+        S(4, 0, 2, 0)
+        SIG(0, 1, 16)
+        SIG(1, 1, 17)
+        Q("b3")
+        C("a3", "v")
+        ADD(5)
+        PJ(6, 1)
+        S(5, 0, 2, 3)
+        PJ(7, 2)
+        SIG(2, 1, 18)
+        SIG(3, 1, 19)
+        Q("a3")
+        ADD(6)
+        SIG(4, 0, 12)
+        SIG(5, 0, 13)
+        S(6, 0, 2, 4)
+        S(7, 0, 2, 5)
+        ADD(7)
+        PQ(2)
+        PQ(3)
+        SIG(6, 0, 14)
+        S(0, 2, 2, 7)
+        S(1, 2, 2, 6)
+        S(2, 2, 2, 1)
+        S(3, 2, 2, 0)
+        SIG(7, 0, 15)
+        nc.vector.tensor_tensor(out=acc0[:, 0:4], in0=acc[:, 8:12], in1=acc[:, 16:20], op=ALU.add)
+        nc.vector.tensor_scalar(out=acc0[:, 0:4], in0=acc0[:, 0:4], scalar1=1.0 / H, scalar2=None, op0=ALU.mult)
+        nc.vector.tensor_scalar(out=acc0[:, 4:8], in0=acc[:, 12:16], scalar1=1.0 / H, scalar2=None, op0=ALU.mult)
+        for r in range(8):
+            SIG(r, 2, r)
+            if r < 4:
+                S(r + 4, 2, 2, r + 2)
+            finish(r)

@@ -162,8 +162,7 @@ def tile_miscore_kernel(tc, y_a, y_b, W, b, out):
             )
             nc.sync.dma_start(out=out_v[:, r, :], in_=o_sb[:, :])
 
-        nc.vector.tensor_copy(out=bias[:, :], in_=b_bf[:, :])
-        for i in range(4):
+        for i in range(5):
             dummy()
         T("w0", 0)
         C("w0", "s", 0)
@@ -174,86 +173,76 @@ def tile_miscore_kernel(tc, y_a, y_b, W, b, out):
         dummy()
         T("b0", 2)
         C("b0", "s", 0)
-        Q("w0")
         C("b0", "s", 1)
+        Q("w0")
         Q("w1")
-        T("a0", 3)
-        C("a0", "s")
-        Q("b0", 0)
-        Q("b0", 1)
-        dummy()
-        T("b1", 6)
-        PJ(0, 4)
-        PJ(1, 5)
+        T("b1", 3)
         C("b1", "s")
-        ADD(0)
-        T("a1", 7)
-        C("a1", "s")
-        T("b2", 0)
+        T("a0", 4)
+        C("a0", "s")
+        Q("b0")
+        dummy()
+        T("b2", 5)
         C("b2", "s")
         Q("b1")
-        ADD(1)
-        PJ(2, 1)
-        PJ(3, 2)
+        PJ(0, 6)
+        PJ(1, 7)
+        PJ(2, 0)
+        PJ(3, 1)
+        nc.vector.tensor_copy(out=bias[:, :], in_=b_bf[:, :])
         Q("a0")
-        PQ(0)
-        S(0, 0, 1, 3)
-        S(1, 0, 1, 4)
-        T("a2", 6)
-        SIG(0, 0, 8)
-        SIG(1, 0, 9)
-        C("a2", "s")
-        Q("a1")
-        ADD(2)
-        S(2, 0, 1, 5)
-        S(3, 0, 1, 7)
-        SIG(2, 0, 10)
-        SIG(3, 0, 11)
-        Q("b2")
-        ADD(3)
-        T("b3", 0)
+        ADD(0)
+        T("a1", 2)
+        C("a1", "s")
+        T("b3", 3)
         C("b3", "s")
-        PJ(4, 1)
-        PJ(5, 2)
-        T("a3", 6)
-        Q("a2")
+        ADD(1)
+        T("a2", 4)
+        C("a2", "s")
+        ADD(2)
+        PQ(0)
+        ADD(3)
+        T("a3", 5)
+        Q("b2")
         PQ(1)
-        ADD(4)
-        S(0, 1, 1, 3)
-        S(1, 1, 1, 4)
-        S(2, 1, 1, 5)
-        S(3, 1, 1, 7)
-        S(4, 0, 2, 0)
-        SIG(0, 1, 16)
-        SIG(1, 1, 17)
+        S(0, 0, 2, 6)
+        S(1, 0, 2, 7)
+        SIG(0, 0, 8)
+        PJ(4, 0)
+        Q("a1")
+        S(2, 0, 2, 1)
         Q("b3")
+        SIG(1, 0, 9)
+        PJ(5, 2)
+        S(3, 0, 2, 3)
+        Q("a2")
+        SIG(2, 0, 10)
         C("a3", "v")
+        ADD(4)
+        PJ(6, 4)
+        S(4, 0, 2, 6)
+        PJ(7, 0)
+        S(5, 0, 2, 7)
+        SIG(3, 0, 11)
         ADD(5)
-        PJ(6, 1)
-        S(5, 0, 2, 3)
-        PJ(7, 2)
-        SIG(2, 1, 18)
-        SIG(3, 1, 19)
-        Q("a3")
-        ADD(6)
         SIG(4, 0, 12)
+        Q("a3")
+        S(6, 0, 2, 1)
         SIG(5, 0, 13)
-        S(6, 0, 2, 4)
-        S(7, 0, 2, 5)
-        ADD(7)
+        S(7, 0, 2, 3)
+        ADD(6)
         PQ(2)
-        PQ(3)
         SIG(6, 0, 14)
-        S(0, 2, 2, 7)
-        S(1, 2, 2, 6)
-        S(2, 2, 2, 1)
-        S(3, 2, 2, 0)
+        ADD(7)
         SIG(7, 0, 15)
-        nc.vector.tensor_tensor(out=acc0[:, 0:4], in0=acc[:, 8:12], in1=acc[:, 16:20], op=ALU.add)
-        nc.vector.tensor_scalar(out=acc0[:, 0:4], in0=acc0[:, 0:4], scalar1=1.0 / H, scalar2=None, op0=ALU.mult)
-        nc.vector.tensor_scalar(out=acc0[:, 4:8], in0=acc[:, 12:16], scalar1=1.0 / H, scalar2=None, op0=ALU.mult)
+        PQ(3)
+        S(0, 2, 2, 2)
+        S(1, 2, 2, 5)
+        S(2, 2, 2, 4)
+        S(3, 2, 2, 6)
+        nc.vector.tensor_scalar(out=acc0[:, :], in0=acc[:, 8:16], scalar1=1.0 / H, scalar2=None, op0=ALU.mult)
         for r in range(8):
             SIG(r, 2, r)
             if r < 4:
-                S(r + 4, 2, 2, r + 2)
+                S(r + 4, 2, 2, (7, 0, 1, 3)[r])
             finish(r)

@@ -71,24 +71,31 @@ def tile_miscore_kernel(tc, y_a, y_b, W, b, out):
         def dummy():
             nc.tensor.matmul(out=dmy[:, :], lhsT=zb[:, 0:128], rhs=zb[:, :], start=True, stop=True)
 
-        def T(x, n):
-            bank = bank_tile(n, "t" + x)
+        def T(x, n, half=None):
+            halves = (0, 1) if half is None else (half,)
+            bank = bank_tile(n, "t%s%s" % (x, "" if half is None else half))
             s32 = srcs[x][:, :].bitcast(F32)
-            for q in range(4):
-                c0 = 256 * (q // 2) + q % 2
-                nc.tensor.transpose(bank[:, 128 * q : 128 * (q + 1)], s32[:, c0 : c0 + 255 : 2], ident[:, :])
-            tp[x] = bank
+            for i, r in enumerate(halves):
+                for u in range(2):
+                    nc.tensor.transpose(
+                        bank[:, 256 * i + 128 * u : 256 * i + 128 * (u + 1)],
+                        s32[:, 256 * r + u : 256 * (r + 1) : 2],
+                        ident[:, :],
+                    )
+                tp[x, r] = bank[:, 256 * i : 256 * (i + 1)]
+            if half is None:
+                tp[x] = bank[:, :]
 
-        def C(x, eng, *halves):
+        def C(x, eng, half=None):
             if x not in gr:
                 gr[x] = keep.tile([P, 1024], BF16, name="g" + x, align_bytes=64)
-            for r0, r1 in [(h, h + 1) for h in halves] or [(0, 2)]:
-                dst = gr[x][:, 512 * r0 : 512 * r1].bitcast(F32).rearrange("p (r c u) -> p r c u", c=128, u=2)
-                src = tp[x][:, 256 * r0 : 256 * r1].rearrange("p (r u c) -> p r c u", u=2, c=128)
-                if eng == "v":
-                    nc.vector.tensor_copy(out=dst, in_=src)
-                else:
-                    nc.scalar.copy(out=dst, in_=src)
+            g, bank = (gr[x][:, :], tp[x]) if half is None else (gr[x][:, 512 * half : 512 * (half + 1)], tp[x, half])
+            dst = g.bitcast(F32).rearrange("p (r c u) -> p r c u", c=128, u=2)
+            src = bank.rearrange("p (r u c) -> p r c u", u=2, c=128)
+            if eng == "v":
+                nc.vector.tensor_copy(out=dst, in_=src)
+            else:
+                nc.scalar.copy(out=dst, in_=src)
 
         def Q(x, *halves):
             if x not in qz:
@@ -165,16 +172,14 @@ def tile_miscore_kernel(tc, y_a, y_b, W, b, out):
         for i in range(5):
             dummy()
         T("w0", 0)
-        C("w0", "s", 0)
-        C("w0", "s", 1)
+        C("w0", "v")
         T("w1", 1)
-        C("w1", "v", 0)
-        C("w1", "v", 1)
+        C("w1", "s")
         dummy()
         T("b0", 2)
-        C("b0", "s", 0)
-        C("b0", "s", 1)
+        C("b0", "s")
         Q("w0")
+        nc.vector.tensor_copy(out=bias[:, :], in_=b_bf[:, :])
         Q("w1")
         T("b1", 3)
         C("b1", "s")
@@ -189,7 +194,6 @@ def tile_miscore_kernel(tc, y_a, y_b, W, b, out):
         PJ(1, 7)
         PJ(2, 0)
         PJ(3, 1)
-        nc.vector.tensor_copy(out=bias[:, :], in_=b_bf[:, :])
         Q("a0")
         ADD(0)
         T("a1", 2)
@@ -200,8 +204,8 @@ def tile_miscore_kernel(tc, y_a, y_b, W, b, out):
         T("a2", 4)
         C("a2", "s")
         ADD(2)
-        PQ(0)
         ADD(3)
+        PQ(0)
         T("a3", 5)
         Q("b2")
         PQ(1)
@@ -231,9 +235,9 @@ def tile_miscore_kernel(tc, y_a, y_b, W, b, out):
         SIG(5, 0, 13)
         S(7, 0, 2, 3)
         ADD(6)
+        ADD(7)
         PQ(2)
         SIG(6, 0, 14)
-        ADD(7)
         SIG(7, 0, 15)
         PQ(3)
         S(0, 2, 2, 2)

@@ -169,7 +169,7 @@ def tile_miscore_kernel(tc, y_a, y_b, W, b, out):
             )
             nc.sync.dma_start(out=out_v[:, r, :], in_=o_sb[:, :])
 
-        for i in range(5):
+        for i in range(7):
             dummy()
         T("w0", 0)
         C("w0", "v")
@@ -207,8 +207,8 @@ def tile_miscore_kernel(tc, y_a, y_b, W, b, out):
         ADD(3)
         PQ(0)
         T("a3", 5)
-        Q("b2")
         PQ(1)
+        Q("b2")
         S(0, 0, 2, 6)
         S(1, 0, 2, 7)
         SIG(0, 0, 8)

from contextlib import ExitStack

import concourse.mybir as mybir
from concourse.masks import make_identity

F32 = mybir.dt.float32
BF16 = mybir.dt.bfloat16
U32 = mybir.dt.uint32
U8 = mybir.dt.uint8
FP8X4 = mybir.dt.float8_e4m3fn_x4
ACT = mybir.ActivationFunctionType
ALU = mybir.AluOpType

P = 128
NA, NB, H = 1024, 1024, 512
FLOPS = 2 * NB * H * H + 2 * NA * NB * H


def tile_miscore_kernel(tc, y_a, y_b, W, b, out):
    nc = tc.nc
    with ExitStack() as ctx:
        keep = ctx.enter_context(tc.tile_pool(name="keep", bufs=1))
        outp = ctx.enter_context(tc.tile_pool(name="outp", bufs=8))
        psum = ctx.enter_context(tc.psum_pool(name="psum", bufs=1))
        ctx.enter_context(tc.manual_schedule())

        ya_v = y_a.rearrange("(p r) o -> p r o", r=8)
        out_v = out.rearrange("(p r) k -> p r k", r=8)
        W_v = W.rearrange("(p t) i -> p t i", t=4)

        def load(name, rows, source):
            x = keep.tile([P, 512 * rows], BF16, name=name)
            nc.sync.dma_start(out=x[:, :].rearrange("p (r k) -> p r k", r=rows), in_=source)
            return x

        b_bf = keep.tile([P, 4], BF16, name="b_bf")
        nc.scalar.dma_start(out=b_bf[:, :], in_=b.rearrange("(p t) -> p t", t=4))
        yb_v = [y_b[256 * c : 256 * (c + 1), :].rearrange("(p r) i -> p r i", r=2) for c in range(4)]
        srcs = {}
        for x, source in (
            ("w0", W_v[:, 0:2, :]), ("w1", W_v[:, 2:4, :]), ("b0", yb_v[0]), ("a0", ya_v[:, 0:2, :]), ("b1", yb_v[1]),
            ("a1", ya_v[:, 2:4, :]), ("b2", yb_v[2]), ("a2", ya_v[:, 4:6, :]), ("b3", yb_v[3]), ("a3", ya_v[:, 6:8, :]),
        ):
            srcs[x] = load(x, 2, source)

        zb = keep.tile([P, 512], BF16, name="zb")
        nc.vector.memset(zb[:, :], 0.0)
        warm = keep.tile([P, 1], F32, name="warm")
        warm2 = keep.tile([P, 1], F32, name="warm2")
        nc.vector.memset(warm[:, :], 0.0)
        nc.scalar.activation(out=warm2[:, :], in_=warm[:, :], func=ACT.Sigmoid)
        ident = keep.tile([P, P], F32, name="ident")
        make_identity(nc, ident[:, :])
        cdiv = keep.tile([P, H], F32, name="cdiv")
        nc.vector.memset(cdiv[:, :], 1.0 / H)
        bias = keep.tile([P, 4], F32, name="bias")
        bias_b = bias[:, :].unsqueeze(1).to_broadcast([P, P, 4])
        acc = keep.tile([P, 20], F32, name="acc")
        acc0 = keep.tile([P, 8], F32, name="acc0")
        junk = keep.tile([P, 512], BF16, name="junk")
        pc = keep.tile([P, NB], U32, name="pc", align_bytes=64)
        ps = keep.tile([P, NB], U8, name="ps", align_bytes=64)
        tp, gr, qz, pj, sc = {}, {}, {}, {}, {}
        g2 = {}

        def bank_tile(n, name):
            return psum.tile([P, 512], F32, name=name, tag="bank%d" % n)

        dmy = bank_tile(7, "dmy")

        def dummy():
            nc.tensor.matmul(out=dmy[:, :], lhsT=zb[:, 0:128], rhs=zb[:, :], start=True, stop=True)

        def T(x, n, half=None):
            halves = (0, 1) if half is None else (half,)
            bank = bank_tile(n, "t%s%s" % (x, "" if half is None else half))
            s32 = srcs[x][:, :].bitcast(F32)
            for i, r in enumerate(halves):
                for u in range(2):
                    nc.tensor.transpose(
                        bank[:, 256 * i + 128 * u : 256 * i + 128 * (u + 1)],
                        s32[:, 256 * r + u : 256 * (r + 1) : 2],
                        ident[:, :],
                    )
                tp[x, r] = bank[:, 256 * i : 256 * (i + 1)]
            if half is None:
                tp[x] = bank[:, :]

        def C(x, eng, half=None):
            if x not in gr:
                gr[x] = keep.tile([P, 1024], BF16, name="g" + x, align_bytes=64)
            g, bank = (gr[x][:, :], tp[x]) if half is None else (gr[x][:, 512 * half : 512 * (half + 1)], tp[x, half])
            dst = g.bitcast(F32).rearrange("p (r c u) -> p r c u", c=128, u=2)
            src = bank.rearrange("p (r u c) -> p r c u", u=2, c=128)
            if eng == "v":
                nc.vector.tensor_copy(out=dst, in_=src)
            else:
                nc.scalar.copy(out=dst, in_=src)

        def Q(x, *halves):
            if x not in qz:
                codes = keep.tile([P, 256], U32, name="c" + x, align_bytes=64)
                scales = keep.tile([P, 256], U8, name="s" + x, align_bytes=64)
                qz[x] = (codes, scales)
            codes, scales = qz[x]
            for r0, r1 in [(h, h + 1) for h in halves] or [(0, 2)]:
                cs = slice(128 * r0, 128 * r1)
                nc.vector.quantize_mx(
                    out=codes[:, cs].bitcast(FP8X4), scales=scales[:, cs], in_=gr[x][:, 512 * r0 : 512 * r1]
                )

        def cols(op, k):
            codes, scales = op
            return codes[:, 128 * k : 128 * (k + 1)].bitcast(FP8X4), scales[:, 128 * k : 128 * (k + 1)]

        def PJ(jc, n):
            bank = bank_tile(n, "pj%d" % jc)
            rhs, rhs_s = cols(qz["b%d" % (jc // 2)], jc % 2)
            for t in range(4):
                lhsT, lhsT_s = cols(qz["w%d" % (t // 2)], t % 2)
                nc.tensor.matmul_mx(
                    out=bank[:, 128 * t : 128 * (t + 1)],
                    lhsT=lhsT, lhsT_scale=lhsT_s, rhs=rhs, rhs_scale=rhs_s,
                    start=True, stop=True,
                )
            pj[jc] = bank

        def ADD(jc):
            c, k = jc // 2, jc % 2
            if k == 0:
                g2[c] = keep.tile([P, 1024], BF16, name="g2c%d" % c, align_bytes=64)
            nc.vector.tensor_tensor(
                out=g2[c][:, 512 * k : 512 * (k + 1)].rearrange("p (j t) -> p j t", t=4),
                in0=pj[jc][:, :].rearrange("p (t j) -> p j t", t=4),
                in1=bias_b,
                op=ALU.add,
            )

        def PQ(c):
            nc.vector.quantize_mx(
                out=pc[:, 256 * c : 256 * (c + 1)].bitcast(FP8X4),
                scales=ps[:, 256 * c : 256 * (c + 1)],
                in_=g2[c][:, :],
            )

        def S(r, c, w, n):
            bank = bank_tile(n, "sc%d_%d" % (r, c))
            lhsT, lhsT_s = cols(qz["a%d" % (r // 2)], r % 2)
            nc.tensor.matmul_mx(
                out=bank[:, 0 : 256 * w], lhsT=lhsT, lhsT_scale=lhsT_s,
                rhs=pc[:, 256 * c : 256 * (c + w)].bitcast(FP8X4), rhs_scale=ps[:, 256 * c : 256 * (c + w)],
                start=True, stop=True,
            )
            sc[(r, c)] = (bank, w)

        def SIG(r, c, col):
            bank, w = sc[(r, c)]
            nc.scalar.activation(
                out=junk[:, 0 : 256 * w], in_=bank[:, 0 : 256 * w], func=ACT.Sigmoid,
                accum_out=acc[:, col : col + 1],
            )

        def finish(r):
            o_sb = outp.tile([P, H], F32, name="o_sb")
            nc.vector.tensor_scalar(
                out=o_sb[:, :], in0=cdiv[:, :],
                scalar1=acc[:, r : r + 1], scalar2=acc0[:, r : r + 1],
                op0=ALU.mult, op1=ALU.add,
            )
            nc.sync.dma_start(out=out_v[:, r, :], in_=o_sb[:, :])

        for i in range(7):
            dummy()
        T("w0", 0)
        C("w0", "v")
        T("w1", 1)
        C("w1", "s")
        dummy()
        T("b0", 2)
        C("b0", "s")
        Q("w0")
        nc.vector.tensor_copy(out=bias[:, :], in_=b_bf[:, :])
        Q("w1")
        T("b1", 3)
        C("b1", "s")
        T("a0", 4)
        C("a0", "s")
        Q("b0")
        dummy()
        T("b2", 5)
        C("b2", "s")
        Q("b1")
        PJ(0, 6)
        PJ(1, 7)
        PJ(2, 0)
        PJ(3, 1)
        Q("a0")
        ADD(0)
        T("a1", 2)
        C("a1", "s")
        T("b3", 3)
        C("b3", "s")
        ADD(1)
        T("a2", 4)
        C("a2", "s")
        ADD(2)
        ADD(3)
        PQ(0)
        T("a3", 5)
        PQ(1)
        Q("b2")
        S(0, 0, 2, 6)
        S(1, 0, 2, 7)
        SIG(0, 0, 8)
        PJ(4, 0)
        Q("a1")
        S(2, 0, 2, 1)
        Q("b3")
        SIG(1, 0, 9)
        PJ(5, 2)
        S(3, 0, 2, 3)
        Q("a2")
        SIG(2, 0, 10)
        C("a3", "v")
        ADD(4)
        PJ(6, 4)
        S(4, 0, 2, 6)
        PJ(7, 0)
        S(5, 0, 2, 7)
        SIG(3, 0, 11)
        ADD(5)
        SIG(4, 0, 12)
        Q("a3")
        S(6, 0, 2, 1)
        SIG(5, 0, 13)
        S(7, 0, 2, 3)
        ADD(6)
        ADD(7)
        PQ(2)
        SIG(6, 0, 14)
        SIG(7, 0, 15)
        PQ(3)
        S(0, 2, 2, 2)
        S(1, 2, 2, 5)
        S(2, 2, 2, 4)
        S(3, 2, 2, 6)
        nc.vector.tensor_scalar(out=acc0[:, :], in0=acc[:, 8:16], scalar1=1.0 / H, scalar2=None, op0=ALU.mult)
        for r in range(8):
            SIG(r, 2, r)
            if r < 4:
                S(r + 4, 2, 2, (7, 0, 1, 3)[r])
            finish(r)
